import numpy as np
import ml_dtypes


def mxq(x, axis, fmt="e4m3"):
    dtype, down = {"e4m3": (ml_dtypes.float8_e4m3fn, 7), "e5m2": (ml_dtypes.float8_e5m2, 14)}[fmt]
    v = np.moveaxis(np.asarray(x, np.float32).astype(ml_dtypes.bfloat16).astype(np.float64), axis, -1)
    blocks = v.reshape(v.shape[:-1] + (-1, 32))
    amax = np.abs(blocks).max(-1, keepdims=True)
    byte = np.maximum(np.where(amax > 0, np.frexp(amax)[1] - 1 + 127, 0) - down, 1)
    scale = np.exp2(byte - 127.0)
    codes = (blocks / scale).astype(np.float32).astype(dtype).astype(np.float64)
    return np.moveaxis((codes * scale).reshape(v.shape), -1, axis)


WIDE = False


def mx_kscale(k):
    if not WIDE:
        return np.ones(k)
    levels = np.array([10, -10, 5, -5, 0])
    a = np.random.permutation(np.resize(levels, k // 512 * 4)).reshape(k // 512, 4)
    idx = np.arange(k)
    return np.exp2(a[idx // 512, idx % 128 // 32])


BF16 = ml_dtypes.bfloat16


def bf(x):
    return np.asarray(x, np.float32).astype(BF16)


def f64(x):
    return np.asarray(x).astype(np.float64)


B, I, H, P = 512, 16128, 256, 2048
C = I + H


def sigmoid(v):
    return 1.0 / (1.0 + np.exp(-v))


def setup_inputs():
    s = mx_kscale(C)
    return {"x": bf(np.random.standard_normal((B, I)) * s[:I]),
            "rh": bf(np.random.standard_normal((B, H)) * 0.95 * s[I:]),
            "update": bf(np.random.standard_normal((B, H)) * 0.7),
            "hidden": bf(1.5 + np.random.standard_normal((B, H))),
            "Wn": bf(np.random.standard_normal((H, C)) / np.sqrt(C) / s[None, :]),
            "bn": bf(-0.1 + 0.2 * np.random.standard_normal(H)),
            "connection_strength": bf(1.0 + 0.3 * np.random.standard_normal(H)),
            "connection_decay": bf(0.4 + 0.2 * np.random.random(1)),
            "connection_history": bf(2.0 * np.random.standard_normal(H))}


def reference(x, rh, update, hidden, Wn, bn, connection_strength, connection_decay, connection_history):
    h = f64(hidden)
    u = f64(update)
    activity = np.mean(np.abs(h), axis=0)
    ch = f64(connection_history) * f64(connection_decay) + activity
    cs = f64(connection_strength) * sigmoid(ch)
    combined_reset = np.concatenate([f64(x), f64(rh)], axis=1)
    new = (mxq(combined_reset, 1, "e4m3") @ mxq(f64(Wn), 1, "e4m3").T) + f64(bn)
    return (1.0 - u) * h + u * new * cs[None, :]

@@ -1,0 +1,245 @@
+from contextlib import ExitStack
+
+import concourse.mybir as mybir
+from concourse.masks import make_identity
+
+FLOPS = 2 * 512 * 256 * 16384
+
+F32 = mybir.dt.float32
+BF16 = mybir.dt.bfloat16
+U32 = mybir.dt.uint32
+U8 = mybir.dt.uint8
+FP8X4 = mybir.dt.float8_e4m3fn_x4
+ALU = mybir.AluOpType
+ACT = mybir.ActivationFunctionType
+
+P = 128
+K_PASS = 512
+K_BLOCK = 256
+BANK = 512
+CHUNK = 4096
+PASSES = CHUNK // K_PASS
+BANKS = CHUNK // (4 * K_BLOCK)
+Q_COLS = 2048
+RAW_BUFS = 12
+
+
+def tile_persistentgrucell_pb_k_kernel(
+    tc,
+    x,
+    rh,
+    update,
+    hidden,
+    Wn,
+    bn,
+    connection_strength,
+    connection_decay,
+    connection_history,
+    out,
+):
+    nc = tc.nc
+    B, I = x.shape
+    H = rh.shape[1]
+    K = I + H
+    ROW_TILES = B // P
+    W_TILES = H // P
+    n_chunks = K // CHUNK
+    assert n_chunks > 3
+
+    x_rows = x.rearrange("(p t) k -> t p k", t=ROW_TILES)
+    out_rows = out.rearrange("(p t) h -> t p h", t=ROW_TILES)
+
+    units = []
+    for c in range(n_chunks):
+        units.extend([("w", c, j) for j in range(W_TILES)])
+        units.extend([("x", c, t) for t in range(ROW_TILES)])
+    n_units = len(units)
+
+    with ExitStack() as ctx:
+        ctx.enter_context(tc.manual_schedule())
+        const = ctx.enter_context(tc.tile_pool(name="const", bufs=1))
+        raw_pool = ctx.enter_context(tc.tile_pool(name="raw", bufs=RAW_BUFS))
+        x_pool = ctx.enter_context(tc.tile_pool(name="xq", bufs=3))
+        w_group_pool = ctx.enter_context(tc.tile_pool(name="wg", bufs=1))
+        w_pool = ctx.enter_context(tc.tile_pool(name="wq", bufs=2))
+        out_pool = ctx.enter_context(tc.tile_pool(name="outs", bufs=2))
+        acc_pool = ctx.enter_context(tc.psum_pool(name="acc", bufs=1))
+        bank_pool = ctx.enter_context(tc.psum_pool(name="banks", bufs=4))
+
+        def load(unit):
+            kind, c, r = unit
+            raw = raw_pool.tile([P, CHUNK], BF16, tag="raw")
+            k0 = c * CHUNK
+            if kind == "w":
+                nc.sync.dma_start(out=raw[:], in_=Wn[r * P : (r + 1) * P, k0 : k0 + CHUNK])
+            else:
+                width = min(CHUNK, I - k0)
+                nc.sync.dma_start(out=raw[:, 0:width], in_=x_rows[r][:, k0 : k0 + width])
+            return raw
+
+        ident = const.tile([P, P], F32)
+        make_identity(nc, ident[:])
+        ones = const.tile([P, P], BF16)
+        nc.vector.memset(ones[:], 1.0)
+        vectors = const.tile([P, 2 * BANK], BF16)
+        nc.vector.memset(vectors[:], 0.0)
+        zero = const.tile([P, 1], F32)
+        nc.vector.memset(zero[:], 0.0)
+
+        raws = {}
+        for i in range(2):
+            raws[i] = load(units[i])
+        hid = const.tile([P, ROW_TILES * H], BF16)
+        nc.scalar.dma_start(out=hid[:], in_=hidden.rearrange("(p t) h -> p (t h)", t=ROW_TILES))
+        nc.scalar.dma_start(out=vectors[0:1, 0:H], in_=bn.unsqueeze(0))
+        nc.scalar.dma_start(out=vectors[0:1, H : 2 * H], in_=connection_strength.unsqueeze(0))
+        nc.scalar.dma_start(out=vectors[0:1, BANK : BANK + H], in_=connection_history.unsqueeze(0))
+        nc.scalar.dma_start(
+            out=vectors[0:1, BANK + H : BANK + H + 1], in_=connection_decay.unsqueeze(0)
+        )
+        upd = const.tile([P, ROW_TILES * H], BF16)
+        nc.scalar.dma_start(out=upd[:], in_=update.rearrange("(p t) h -> p (t h)", t=ROW_TILES))
+        for i in range(2, RAW_BUFS):
+            raws[i] = load(units[i])
+        rh_sb = const.tile([P, ROW_TILES * H], BF16)
+        nc.sync.dma_start(out=rh_sb[:], in_=rh.rearrange("(p t) c -> p (t c)", t=ROW_TILES))
+
+        warm = const.tile([P, 1], F32)
+        nc.scalar.activation(out=warm[:], in_=zero[:], func=ACT.Sigmoid)
+
+        habs = const.tile([P, ROW_TILES * H], BF16)
+        nc.vector.scalar_tensor_tensor(
+            out=habs[:], in0=hid[:], scalar=-1.0, in1=hid[:], op0=ALU.mult, op1=ALU.max
+        )
+        spread_a = acc_pool.tile([P, BANK], F32, tag="acc0")
+        nc.tensor.matmul(spread_a[:], lhsT=ones[:], rhs=vectors[:, 0:BANK], start=True, stop=True)
+        spread_b = acc_pool.tile([P, BANK], F32, tag="acc1")
+        nc.tensor.matmul(
+            spread_b[:], lhsT=ones[:], rhs=vectors[:, BANK : 2 * BANK], start=True, stop=True
+        )
+        abs_sum = acc_pool.tile([P, H], F32, tag="acc2")
+        for t in range(ROW_TILES):
+            nc.tensor.matmul(
+                abs_sum[:],
+                lhsT=ones[:],
+                rhs=habs[:, t * H : (t + 1) * H],
+                start=(t == 0),
+                stop=(t == ROW_TILES - 1),
+            )
+        keep = const.tile([P, ROW_TILES * H], F32)
+        nc.vector.tensor_tensor(out=keep[:], in0=upd[:], in1=hid[:], op=ALU.mult)
+        nc.vector.tensor_tensor(out=keep[:], in0=hid[:], in1=keep[:], op=ALU.subtract)
+        decay = const.tile([P, 1], F32)
+        nc.vector.tensor_copy(out=decay[:], in_=spread_b[:, H : H + 1])
+        ch = const.tile([P, H], F32)
+        nc.vector.tensor_scalar(
+            out=ch[:], in0=spread_b[:, 0:H], scalar1=decay[:, 0:1], scalar2=None, op0=ALU.mult
+        )
+        nc.vector.scalar_tensor_tensor(
+            out=ch[:], in0=abs_sum[:], scalar=1.0 / B, in1=ch[:], op0=ALU.mult, op1=ALU.add
+        )
+        sig = const.tile([P, H], F32)
+        nc.scalar.activation(out=sig[:], in_=ch[:], func=ACT.Sigmoid)
+        cs = const.tile([P, H], F32)
+        nc.vector.tensor_tensor(out=cs[:], in0=sig[:], in1=spread_a[:, H : 2 * H], op=ALU.mult)
+        cs_bn = const.tile([P, H], F32)
+        nc.vector.tensor_tensor(out=cs_bn[:], in0=cs[:], in1=spread_a[:, 0:H], op=ALU.mult)
+
+        gain = const.tile([P, ROW_TILES * H], F32)
+        bias = const.tile([P, ROW_TILES * H], F32)
+
+        def prepare_blend(step, t):
+            cols = slice(t * H, (t + 1) * H)
+            if step == 0:
+                nc.vector.tensor_tensor(out=gain[:, cols], in0=upd[:, cols], in1=cs[:], op=ALU.mult)
+            elif step == 1:
+                nc.vector.tensor_tensor(out=bias[:, cols], in0=upd[:, cols], in1=cs_bn[:], op=ALU.mult)
+            elif step == 2:
+                nc.vector.tensor_tensor(
+                    out=keep[:, cols], in0=keep[:, cols], in1=bias[:, cols], op=ALU.add
+                )
+
+        acc = [
+            acc_pool.tile([P, H], F32, name="acc%d" % t, tag="acc%d" % t) for t in range(ROW_TILES)
+        ]
+
+        def transpose_and_regroup(blocks, grouped):
+            for b in range(BANKS):
+                bank = bank_pool.tile([P, BANK], F32, tag="bank")
+                for q in range(4):
+                    nc.tensor.transpose(bank[:, q * P : (q + 1) * P], blocks[4 * b + q], ident[:])
+                regrouped = bank[:].rearrange("p (g u r) -> p g r u", g=2, u=2)
+                if b == 0:
+                    nc.vector.tensor_copy(out=grouped[:, 2 * b : 2 * b + 2], in_=regrouped)
+                else:
+                    nc.scalar.copy(out=grouped[:, 2 * b : 2 * b + 2], in_=regrouped)
+
+        def quantise(grouped, codes, scales):
+            for s in range(grouped.shape[1] // Q_COLS):
+                nc.vector.quantize_mx(
+                    out=codes[:, s * Q_COLS // 4 : (s + 1) * Q_COLS // 4].bitcast(FP8X4),
+                    scales=scales[:, s * Q_COLS // 4 : (s + 1) * Q_COLS // 4],
+                    in_=grouped[:, s * Q_COLS : (s + 1) * Q_COLS],
+                )
+
+        def multiply(c, t, x_codes, x_scales, w_codes, w_scales):
+            for g in range(PASSES):
+                nc.tensor.matmul_mx(
+                    out=acc[t][:],
+                    lhsT=x_codes[:, g * P : (g + 1) * P].bitcast(FP8X4),
+                    lhsT_scale=x_scales[:, g * P : (g + 1) * P],
+                    rhs=w_codes[:, g * H : (g + 1) * H].bitcast(FP8X4),
+                    rhs_scale=w_scales[:, g * H : (g + 1) * H],
+                    start=(c == 0 and g == 0),
+                    stop=(c == n_chunks - 1 and g == PASSES - 1),
+                )
+
+        def blend_and_store(t):
+            cols = slice(t * H, (t + 1) * H)
+            result = out_pool.tile([P, H], F32, tag="result")
+            nc.vector.tensor_tensor(out=result[:], in0=acc[t][:], in1=gain[:, cols], op=ALU.mult)
+            nc.vector.tensor_tensor(out=result[:], in0=result[:], in1=keep[:, cols], op=ALU.add)
+            nc.sync.dma_start(out=out_rows[t], in_=result[:])
+
+        waiting = None
+        for i in range(n_units + 1):
+            if i < n_units:
+                kind, c, r = units[i]
+                words = raws[i][:].bitcast(F32)
+                blocks = [words[:, q * P : (q + 1) * P] for q in range(CHUNK // K_BLOCK)]
+                if kind == "x" and (c + 1) * CHUNK > I:
+                    blocks[-1] = rh_sb[:].bitcast(F32)[:, r * P : (r + 1) * P]
+                if kind == "w":
+                    if r == 0:
+                        w_grouped = w_group_pool.tile([P, W_TILES * CHUNK], BF16, align_bytes=64)
+                    grouped_view = w_grouped[:].bitcast(F32).rearrange(
+                        "p (g j r u) -> p g j r u", g=PASSES, j=W_TILES, u=2
+                    )[:, :, r]
+                else:
+                    x_grouped = x_pool.tile([P, CHUNK], BF16, align_bytes=64)
+                    grouped_view = x_grouped[:].bitcast(F32).rearrange(
+                        "p (g r u) -> p g r u", g=PASSES, u=2
+                    )
+                transpose_and_regroup(blocks, grouped_view)
+                if i + RAW_BUFS < n_units:
+                    raws[i + RAW_BUFS] = load(units[i + RAW_BUFS])
+
+            if waiting is not None:
+                multiply(*waiting, w_codes, w_scales)
+
+            if i < n_units and kind == "w" and r == W_TILES - 1:
+                new_w_codes = w_pool.tile([P, W_TILES * CHUNK // 4], U32, align_bytes=64)
+                new_w_scales = w_pool.tile([P, W_TILES * CHUNK // 4], U8, align_bytes=64)
+                quantise(w_grouped, new_w_codes, new_w_scales)
+            if i < n_units and kind == "x":
+                x_codes = x_pool.tile([P, CHUNK // 4], U32, align_bytes=64)
+                x_scales = x_pool.tile([P, CHUNK // 4], U8, align_bytes=64)
+                quantise(x_grouped, x_codes, x_scales)
+                prepare_blend(c, r)
+
+            if waiting is not None and waiting[0] == n_chunks - 1:
+                blend_and_store(waiting[1])
+
+            if i < n_units and kind == "w" and r == W_TILES - 1:
+                w_codes, w_scales = new_w_codes, new_w_scales
+            waiting = (c, r, x_codes, x_scales) if (i < n_units and kind == "x") else None

@@ -17,10 +17,16 @@ P = 128
 K_PASS = 512
 K_BLOCK = 256
 BANK = 512
+K_BANK = 4 * K_BLOCK
 CHUNK = 4096
-PASSES = CHUNK // K_PASS
-BANKS = CHUNK // (4 * K_BLOCK)
-Q_COLS = 2048
+UNIT_BANKS = CHUNK // K_BANK
+CHUNK_PASSES = CHUNK // K_PASS
+STEP_K = 2048
+STEP_PASSES = STEP_K // K_PASS
+X_BANKS = STEP_K // K_BANK
+W_BANKS = X_BANKS // 2
+STEPS_PER_UNIT = CHUNK // STEP_K
+LAG = 2
 RAW_BUFS = 12
 
 
@@ -45,23 +51,31 @@ def tile_persistentgrucell_pb_k_kernel(
     W_TILES = H // P
     n_chunks = K // CHUNK
     assert n_chunks > 3
+    assert ROW_TILES * STEPS_PER_UNIT * W_BANKS == W_TILES * UNIT_BANKS
 
     x_rows = x.rearrange("(p t) k -> t p k", t=ROW_TILES)
     out_rows = out.rearrange("(p t) h -> t p h", t=ROW_TILES)
 
-    units = []
+    stream = [("w", 0, j) for j in range(W_TILES)]
     for c in range(n_chunks):
-        units.extend([("w", c, j) for j in range(W_TILES)])
-        units.extend([("x", c, t) for t in range(ROW_TILES)])
-    n_units = len(units)
+        for j in range(W_TILES):
+            if c + 1 < n_chunks:
+                stream.append(("w", c + 1, j))
+            stream.extend([("x", c, t) for t in range(2 * j, 2 * j + 2)])
+    position = dict([(unit, n) for n, unit in enumerate(stream)])
+
+    steps = []
+    for c in range(n_chunks):
+        for t in range(ROW_TILES):
+            steps.extend([(c, t, h) for h in range(STEPS_PER_UNIT)])
+    n_steps = len(steps)
 
     with ExitStack() as ctx:
         ctx.enter_context(tc.manual_schedule())
         const = ctx.enter_context(tc.tile_pool(name="const", bufs=1))
         raw_pool = ctx.enter_context(tc.tile_pool(name="raw", bufs=RAW_BUFS))
-        x_pool = ctx.enter_context(tc.tile_pool(name="xq", bufs=3))
-        w_group_pool = ctx.enter_context(tc.tile_pool(name="wg", bufs=1))
-        w_pool = ctx.enter_context(tc.tile_pool(name="wq", bufs=2))
+        stage = ctx.enter_context(tc.tile_pool(name="stage", bufs=LAG + 2))
+        w_pool = ctx.enter_context(tc.tile_pool(name="wq", bufs=3))
         out_pool = ctx.enter_context(tc.tile_pool(name="outs", bufs=2))
         acc_pool = ctx.enter_context(tc.psum_pool(name="acc", bufs=1))
         bank_pool = ctx.enter_context(tc.psum_pool(name="banks", bufs=4))
@@ -88,7 +102,7 @@ def tile_persistentgrucell_pb_k_kernel(
 
         raws = {}
         for i in range(2):
-            raws[i] = load(units[i])
+            raws[stream[i]] = load(stream[i])
         hid = const.tile([P, ROW_TILES * H], BF16)
         nc.scalar.dma_start(out=hid[:], in_=hidden.rearrange("(p t) h -> p (t h)", t=ROW_TILES))
         nc.scalar.dma_start(out=vectors[0:1, 0:H], in_=bn.unsqueeze(0))
@@ -100,7 +114,7 @@ def tile_persistentgrucell_pb_k_kernel(
         upd = const.tile([P, ROW_TILES * H], BF16)
         nc.scalar.dma_start(out=upd[:], in_=update.rearrange("(p t) h -> p (t h)", t=ROW_TILES))
         for i in range(2, RAW_BUFS):
-            raws[i] = load(units[i])
+            raws[stream[i]] = load(stream[i])
         rh_sb = const.tile([P, ROW_TILES * H], BF16)
         nc.sync.dma_start(out=rh_sb[:], in_=rh.rearrange("(p t) c -> p (t c)", t=ROW_TILES))
 
@@ -163,35 +177,70 @@ def tile_persistentgrucell_pb_k_kernel(
             acc_pool.tile([P, H], F32, name="acc%d" % t, tag="acc%d" % t) for t in range(ROW_TILES)
         ]
 
-        def transpose_and_regroup(blocks, grouped):
-            for b in range(BANKS):
-                bank = bank_pool.tile([P, BANK], F32, tag="bank")
-                for q in range(4):
-                    nc.tensor.transpose(bank[:, q * P : (q + 1) * P], blocks[4 * b + q], ident[:])
-                regrouped = bank[:].rearrange("p (g u r) -> p g r u", g=2, u=2)
-                if b == 0:
-                    nc.vector.tensor_copy(out=grouped[:, 2 * b : 2 * b + 2], in_=regrouped)
-                else:
-                    nc.scalar.copy(out=grouped[:, 2 * b : 2 * b + 2], in_=regrouped)
+        def transpose_bank(blocks, grouped, on_vector):
+            bank = bank_pool.tile([P, BANK], F32, tag="bank")
+            for q in range(4):
+                nc.tensor.transpose(bank[:, q * P : (q + 1) * P], blocks[q], ident[:])
+            regrouped = bank[:].rearrange("p (g u r) -> p g r u", g=2, u=2)
+            words = grouped.bitcast(F32).rearrange("p (g r u) -> p g r u", g=2, u=2)
+            if on_vector:
+                nc.vector.tensor_copy(out=words, in_=regrouped)
+            else:
+                nc.scalar.copy(out=words, in_=regrouped)
 
-        def quantise(grouped, codes, scales):
-            for s in range(grouped.shape[1] // Q_COLS):
+        def blocks_of(unit):
+            kind, c, r = unit
+            words = raws[unit][:].bitcast(F32)
+            blocks = [words[:, q * P : (q + 1) * P] for q in range(CHUNK // K_BLOCK)]
+            if kind == "x" and (c + 1) * CHUNK > I:
+                blocks[-1] = rh_sb[:].bitcast(F32)[:, r * P : (r + 1) * P]
+            return blocks
+
+        def transpose_x(c, t, h):
+            blocks = blocks_of(("x", c, t))[4 * X_BANKS * h : 4 * X_BANKS * (h + 1)]
+            x_grouped = stage.tile([P, STEP_K], BF16, align_bytes=64)
+            for b in range(X_BANKS):
+                transpose_bank(
+                    blocks[4 * b : 4 * b + 4], x_grouped[:, b * K_BANK : (b + 1) * K_BANK], False
+                )
+            return x_grouped
+
+        def transpose_w(c, n):
+            j, b = divmod(n, UNIT_BANKS)
+            w_grouped = stage.tile([P, K_BANK], BF16, align_bytes=64)
+            transpose_bank(blocks_of(("w", c, j))[4 * b : 4 * b + 4], w_grouped[:], n % 2 == 1)
+            return w_grouped
+
+        w_codes = {}
+        w_scales = {}
+
+        def quantise_w(c, n, w_grouped):
+            j, b = divmod(n, UNIT_BANKS)
+            for g in range(2):
+                first = ((2 * b + g) * W_TILES + j) * P
                 nc.vector.quantize_mx(
-                    out=codes[:, s * Q_COLS // 4 : (s + 1) * Q_COLS // 4].bitcast(FP8X4),
-                    scales=scales[:, s * Q_COLS // 4 : (s + 1) * Q_COLS // 4],
-                    in_=grouped[:, s * Q_COLS : (s + 1) * Q_COLS],
+                    out=w_codes[c][:, first : first + P].bitcast(FP8X4),
+                    scales=w_scales[c][:, first : first + P],
+                    in_=w_grouped[:, g * 4 * P : (g + 1) * 4 * P],
                 )
 
-        def multiply(c, t, x_codes, x_scales, w_codes, w_scales):
-            for g in range(PASSES):
+        def quantise_x(x_grouped):
+            x_codes = stage.tile([P, STEP_K // 4], U32, align_bytes=64)
+            x_scales = stage.tile([P, STEP_K // 4], U8, align_bytes=64)
+            nc.vector.quantize_mx(out=x_codes[:].bitcast(FP8X4), scales=x_scales[:], in_=x_grouped[:])
+            return x_codes, x_scales
+
+        def multiply(c, t, h, x_codes, x_scales):
+            for g in range(STEP_PASSES):
+                g_chunk = h * STEP_PASSES + g
                 nc.tensor.matmul_mx(
                     out=acc[t][:],
                     lhsT=x_codes[:, g * P : (g + 1) * P].bitcast(FP8X4),
                     lhsT_scale=x_scales[:, g * P : (g + 1) * P],
-                    rhs=w_codes[:, g * H : (g + 1) * H].bitcast(FP8X4),
-                    rhs_scale=w_scales[:, g * H : (g + 1) * H],
-                    start=(c == 0 and g == 0),
-                    stop=(c == n_chunks - 1 and g == PASSES - 1),
+                    rhs=w_codes[c][:, g_chunk * H : (g_chunk + 1) * H].bitcast(FP8X4),
+                    rhs_scale=w_scales[c][:, g_chunk * H : (g_chunk + 1) * H],
+                    start=(c == 0 and g_chunk == 0),
+                    stop=(c == n_chunks - 1 and g_chunk == CHUNK_PASSES - 1),
                 )
 
         def blend_and_store(t):
@@ -201,45 +250,51 @@ def tile_persistentgrucell_pb_k_kernel(
             nc.vector.tensor_tensor(out=result[:], in0=result[:], in1=keep[:, cols], op=ALU.add)
             nc.sync.dma_start(out=out_rows[t], in_=result[:])
 
-        waiting = None
-        for i in range(n_units + 1):
-            if i < n_units:
-                kind, c, r = units[i]
-                words = raws[i][:].bitcast(F32)
-                blocks = [words[:, q * P : (q + 1) * P] for q in range(CHUNK // K_BLOCK)]
-                if kind == "x" and (c + 1) * CHUNK > I:
-                    blocks[-1] = rh_sb[:].bitcast(F32)[:, r * P : (r + 1) * P]
-                if kind == "w":
-                    if r == 0:
-                        w_grouped = w_group_pool.tile([P, W_TILES * CHUNK], BF16, align_bytes=64)
-                    grouped_view = w_grouped[:].bitcast(F32).rearrange(
-                        "p (g j r u) -> p g j r u", g=PASSES, j=W_TILES, u=2
-                    )[:, :, r]
-                else:
-                    x_grouped = x_pool.tile([P, CHUNK], BF16, align_bytes=64)
-                    grouped_view = x_grouped[:].bitcast(F32).rearrange(
-                        "p (g r u) -> p g r u", g=PASSES, u=2
-                    )
-                transpose_and_regroup(blocks, grouped_view)
-                if i + RAW_BUFS < n_units:
-                    raws[i + RAW_BUFS] = load(units[i + RAW_BUFS])
+        def new_w_tiles(c):
+            codes = w_pool.tile([P, CHUNK_PASSES * H], U32, align_bytes=64, tag="w_codes")
+            scales = w_pool.tile([P, CHUNK_PASSES * H], U8, align_bytes=64, tag="w_scales")
+            w_codes[c] = codes
+            w_scales[c] = scales
 
-            if waiting is not None:
-                multiply(*waiting, w_codes, w_scales)
+        new_w_tiles(0)
+        w_waiting = []
+        for n in range(W_TILES * UNIT_BANKS):
+            w_now = [(0, n, transpose_w(0, n))]
+            for item in w_waiting:
+                quantise_w(*item)
+            w_waiting = w_now
 
-            if i < n_units and kind == "w" and r == W_TILES - 1:
-                new_w_codes = w_pool.tile([P, W_TILES * CHUNK // 4], U32, align_bytes=64)
-                new_w_scales = w_pool.tile([P, W_TILES * CHUNK // 4], U8, align_bytes=64)
-                quantise(w_grouped, new_w_codes, new_w_scales)
-            if i < n_units and kind == "x":
-                x_codes = x_pool.tile([P, CHUNK // 4], U32, align_bytes=64)
-                x_scales = x_pool.tile([P, CHUNK // 4], U8, align_bytes=64)
-                quantise(x_grouped, x_codes, x_scales)
-                prepare_blend(c, r)
+        n_loaded = RAW_BUFS
+        x_waiting = None
+        x_ready = {}
+        for s in range(n_steps + LAG):
+            if x_waiting is not None:
+                x_ready[s - 1] = quantise_x(x_waiting)
+                x_waiting = None
+            for item in w_waiting:
+                quantise_w(*item)
+            w_waiting = []
 
-            if waiting is not None and waiting[0] == n_chunks - 1:
-                blend_and_store(waiting[1])
+            if s < n_steps:
+                c, t, h = steps[s]
+                x_waiting = transpose_x(c, t, h)
+                if c + 1 < n_chunks:
+                    m = t * STEPS_PER_UNIT + h
+                    if m == 0:
+                        new_w_tiles(c + 1)
+                    for n in range(m * W_BANKS, (m + 1) * W_BANKS):
+                        w_waiting.append((c + 1, n, transpose_w(c + 1, n)))
+                if t % 2 == 1 and h == STEPS_PER_UNIT - 1:
+                    n_free = min(len(stream), position[("x", c, t)] + 1 + RAW_BUFS)
+                    for n in range(n_loaded, n_free):
+                        raws[stream[n]] = load(stream[n])
+                    n_loaded = max(n_loaded, n_free)
 
-            if i < n_units and kind == "w" and r == W_TILES - 1:
-                w_codes, w_scales = new_w_codes, new_w_scales
-            waiting = (c, r, x_codes, x_scales) if (i < n_units and kind == "x") else None
+            if s >= LAG:
+                c_old, t_old, h_old = steps[s - LAG]
+                multiply(c_old, t_old, h_old, *x_ready[s - LAG])
+
+            if s < n_steps and h == 0:
+                prepare_blend(c, t)
+            if s >= LAG and c_old == n_chunks - 1 and h_old == STEPS_PER_UNIT - 1:
+                blend_and_store(t_old)

@@ -21,12 +21,12 @@ K_BANK = 4 * K_BLOCK
 CHUNK = 4096
 UNIT_BANKS = CHUNK // K_BANK
 CHUNK_PASSES = CHUNK // K_PASS
-STEP_K = 2048
+STEP_K = 4096
 STEP_PASSES = STEP_K // K_PASS
 X_BANKS = STEP_K // K_BANK
 W_BANKS = X_BANKS // 2
 STEPS_PER_UNIT = CHUNK // STEP_K
-LAG = 2
+LAG = 1
 RAW_BUFS = 12
 
 

@@ -18,16 +18,12 @@ K_PASS = 512
 K_BLOCK = 256
 BANK = 512
 K_BANK = 4 * K_BLOCK
-CHUNK = 4096
-UNIT_BANKS = CHUNK // K_BANK
-CHUNK_PASSES = CHUNK // K_PASS
-STEP_K = 4096
-STEP_PASSES = STEP_K // K_PASS
-X_BANKS = STEP_K // K_BANK
-W_BANKS = X_BANKS // 2
-STEPS_PER_UNIT = CHUNK // STEP_K
-LAG = 1
-RAW_BUFS = 12
+SLAB = 2048
+SLAB_PASSES = SLAB // K_PASS
+UNIT_BANKS = SLAB // K_BANK
+LAG = 2
+LEAD = 2
+RAW_BUFS = 24
 
 
 def tile_persistentgrucell_pb_k_kernel(
@@ -49,26 +45,36 @@ def tile_persistentgrucell_pb_k_kernel(
     K = I + H
     ROW_TILES = B // P
     W_TILES = H // P
-    n_chunks = K // CHUNK
-    assert n_chunks > 3
-    assert ROW_TILES * STEPS_PER_UNIT * W_BANKS == W_TILES * UNIT_BANKS
+    n_slabs = K // SLAB
+    assert n_slabs > 3
 
     x_rows = x.rearrange("(p t) k -> t p k", t=ROW_TILES)
     out_rows = out.rearrange("(p t) h -> t p h", t=ROW_TILES)
 
-    stream = [("w", 0, j) for j in range(W_TILES)]
-    for c in range(n_chunks):
-        for j in range(W_TILES):
-            if c + 1 < n_chunks:
-                stream.append(("w", c + 1, j))
-            stream.extend([("x", c, t) for t in range(2 * j, 2 * j + 2)])
-    position = dict([(unit, n) for n, unit in enumerate(stream)])
-
-    steps = []
-    for c in range(n_chunks):
-        for t in range(ROW_TILES):
-            steps.extend([(c, t, h) for h in range(STEPS_PER_UNIT)])
+    steps = [(slab, t) for slab in range(n_slabs) for t in range(ROW_TILES)]
+    w_banks = [
+        (slab, j, b) for slab in range(n_slabs) for j in range(W_TILES) for b in range(UNIT_BANKS)
+    ]
     n_steps = len(steps)
+    assert len(w_banks) == n_steps
+    assert W_TILES * UNIT_BANKS - 1 - LEAD + 1 <= LAG
+
+    stream = []
+    last_use = {}
+    for i in range(LEAD):
+        slab, j, b = w_banks[i]
+        if b == 0:
+            stream.append(("w", slab, j))
+        last_use[("w", slab, j)] = -1
+    for s in range(n_steps):
+        if s + LEAD < n_steps:
+            slab, j, b = w_banks[s + LEAD]
+            if b == 0:
+                stream.append(("w", slab, j))
+            last_use[("w", slab, j)] = s
+        slab, t = steps[s]
+        stream.append(("x", slab, t))
+        last_use[("x", slab, t)] = s
 
     with ExitStack() as ctx:
         ctx.enter_context(tc.manual_schedule())
@@ -81,13 +87,13 @@ def tile_persistentgrucell_pb_k_kernel(
         bank_pool = ctx.enter_context(tc.psum_pool(name="banks", bufs=4))
 
         def load(unit):
-            kind, c, r = unit
-            raw = raw_pool.tile([P, CHUNK], BF16, tag="raw")
-            k0 = c * CHUNK
+            kind, slab, r = unit
+            raw = raw_pool.tile([P, SLAB], BF16, tag="raw")
+            k0 = slab * SLAB
             if kind == "w":
-                nc.sync.dma_start(out=raw[:], in_=Wn[r * P : (r + 1) * P, k0 : k0 + CHUNK])
+                nc.sync.dma_start(out=raw[:], in_=Wn[r * P : (r + 1) * P, k0 : k0 + SLAB])
             else:
-                width = min(CHUNK, I - k0)
+                width = min(SLAB, I - k0)
                 nc.sync.dma_start(out=raw[:, 0:width], in_=x_rows[r][:, k0 : k0 + width])
             return raw
 
@@ -101,8 +107,7 @@ def tile_persistentgrucell_pb_k_kernel(
         nc.vector.memset(zero[:], 0.0)
 
         raws = {}
-        for i in range(2):
-            raws[stream[i]] = load(stream[i])
+        raws[stream[0]] = load(stream[0])
         hid = const.tile([P, ROW_TILES * H], BF16)
         nc.scalar.dma_start(out=hid[:], in_=hidden.rearrange("(p t) h -> p (t h)", t=ROW_TILES))
         nc.scalar.dma_start(out=vectors[0:1, 0:H], in_=bn.unsqueeze(0))
@@ -111,9 +116,11 @@ def tile_persistentgrucell_pb_k_kernel(
         nc.scalar.dma_start(
             out=vectors[0:1, BANK + H : BANK + H + 1], in_=connection_decay.unsqueeze(0)
         )
+        for i in range(1, 4):
+            raws[stream[i]] = load(stream[i])
         upd = const.tile([P, ROW_TILES * H], BF16)
         nc.scalar.dma_start(out=upd[:], in_=update.rearrange("(p t) h -> p (t h)", t=ROW_TILES))
-        for i in range(2, RAW_BUFS):
+        for i in range(4, RAW_BUFS):
             raws[stream[i]] = load(stream[i])
         rh_sb = const.tile([P, ROW_TILES * H], BF16)
         nc.sync.dma_start(out=rh_sb[:], in_=rh.rearrange("(p t) c -> p (t c)", t=ROW_TILES))
@@ -189,58 +196,60 @@ def tile_persistentgrucell_pb_k_kernel(
                 nc.scalar.copy(out=words, in_=regrouped)
 
         def blocks_of(unit):
-            kind, c, r = unit
+            kind, slab, r = unit
             words = raws[unit][:].bitcast(F32)
-            blocks = [words[:, q * P : (q + 1) * P] for q in range(CHUNK // K_BLOCK)]
-            if kind == "x" and (c + 1) * CHUNK > I:
+            blocks = [words[:, q * P : (q + 1) * P] for q in range(SLAB // K_BLOCK)]
+            if kind == "x" and (slab + 1) * SLAB > I:
                 blocks[-1] = rh_sb[:].bitcast(F32)[:, r * P : (r + 1) * P]
             return blocks
 
-        def transpose_x(c, t, h):
-            blocks = blocks_of(("x", c, t))[4 * X_BANKS * h : 4 * X_BANKS * (h + 1)]
-            x_grouped = stage.tile([P, STEP_K], BF16, align_bytes=64)
-            for b in range(X_BANKS):
+        def transpose_x(slab, t):
+            blocks = blocks_of(("x", slab, t))
+            x_grouped = stage.tile([P, SLAB], BF16, align_bytes=64)
+            for b in range(UNIT_BANKS):
                 transpose_bank(
                     blocks[4 * b : 4 * b + 4], x_grouped[:, b * K_BANK : (b + 1) * K_BANK], False
                 )
             return x_grouped
 
-        def transpose_w(c, n):
-            j, b = divmod(n, UNIT_BANKS)
+        def transpose_w(slab, j, b):
             w_grouped = stage.tile([P, K_BANK], BF16, align_bytes=64)
-            transpose_bank(blocks_of(("w", c, j))[4 * b : 4 * b + 4], w_grouped[:], n % 2 == 1)
+            transpose_bank(blocks_of(("w", slab, j))[4 * b : 4 * b + 4], w_grouped[:], b % 2 == 1)
             return w_grouped
 
         w_codes = {}
         w_scales = {}
 
-        def quantise_w(c, n, w_grouped):
-            j, b = divmod(n, UNIT_BANKS)
+        def quantise_w(slab, j, b, w_grouped):
+            if j == 0 and b == 0:
+                codes = w_pool.tile([P, SLAB_PASSES * H], U32, align_bytes=64, tag="w_codes")
+                scales = w_pool.tile([P, SLAB_PASSES * H], U8, align_bytes=64, tag="w_scales")
+                w_codes[slab] = codes
+                w_scales[slab] = scales
             for g in range(2):
                 first = ((2 * b + g) * W_TILES + j) * P
                 nc.vector.quantize_mx(
-                    out=w_codes[c][:, first : first + P].bitcast(FP8X4),
-                    scales=w_scales[c][:, first : first + P],
+                    out=w_codes[slab][:, first : first + P].bitcast(FP8X4),
+                    scales=w_scales[slab][:, first : first + P],
                     in_=w_grouped[:, g * 4 * P : (g + 1) * 4 * P],
                 )
 
         def quantise_x(x_grouped):
-            x_codes = stage.tile([P, STEP_K // 4], U32, align_bytes=64)
-            x_scales = stage.tile([P, STEP_K // 4], U8, align_bytes=64)
+            x_codes = stage.tile([P, SLAB // 4], U32, align_bytes=64)
+            x_scales = stage.tile([P, SLAB // 4], U8, align_bytes=64)
             nc.vector.quantize_mx(out=x_codes[:].bitcast(FP8X4), scales=x_scales[:], in_=x_grouped[:])
             return x_codes, x_scales
 
-        def multiply(c, t, h, x_codes, x_scales):
-            for g in range(STEP_PASSES):
-                g_chunk = h * STEP_PASSES + g
+        def multiply(slab, t, x_codes, x_scales):
+            for g in range(SLAB_PASSES):
                 nc.tensor.matmul_mx(
                     out=acc[t][:],
                     lhsT=x_codes[:, g * P : (g + 1) * P].bitcast(FP8X4),
                     lhsT_scale=x_scales[:, g * P : (g + 1) * P],
-                    rhs=w_codes[c][:, g_chunk * H : (g_chunk + 1) * H].bitcast(FP8X4),
-                    rhs_scale=w_scales[c][:, g_chunk * H : (g_chunk + 1) * H],
-                    start=(c == 0 and g_chunk == 0),
-                    stop=(c == n_chunks - 1 and g_chunk == CHUNK_PASSES - 1),
+                    rhs=w_codes[slab][:, g * H : (g + 1) * H].bitcast(FP8X4),
+                    rhs_scale=w_scales[slab][:, g * H : (g + 1) * H],
+                    start=(slab == 0 and g == 0),
+                    stop=(slab == n_slabs - 1 and g == SLAB_PASSES - 1),
                 )
 
         def blend_and_store(t):
@@ -250,23 +259,10 @@ def tile_persistentgrucell_pb_k_kernel(
             nc.vector.tensor_tensor(out=result[:], in0=result[:], in1=keep[:, cols], op=ALU.add)
             nc.sync.dma_start(out=out_rows[t], in_=result[:])
 
-        def new_w_tiles(c):
-            codes = w_pool.tile([P, CHUNK_PASSES * H], U32, align_bytes=64, tag="w_codes")
-            scales = w_pool.tile([P, CHUNK_PASSES * H], U8, align_bytes=64, tag="w_scales")
-            w_codes[c] = codes
-            w_scales[c] = scales
-
-        new_w_tiles(0)
-        w_waiting = []
-        for n in range(W_TILES * UNIT_BANKS):
-            w_now = [(0, n, transpose_w(0, n))]
-            for item in w_waiting:
-                quantise_w(*item)
-            w_waiting = w_now
-
-        n_loaded = RAW_BUFS
+        w_waiting = [(slab, j, b, transpose_w(slab, j, b)) for slab, j, b in w_banks[0:LEAD]]
         x_waiting = None
         x_ready = {}
+        n_loaded = RAW_BUFS
         for s in range(n_steps + LAG):
             if x_waiting is not None:
                 x_ready[s - 1] = quantise_x(x_waiting)
@@ -276,25 +272,20 @@ def tile_persistentgrucell_pb_k_kernel(
             w_waiting = []
 
             if s < n_steps:
-                c, t, h = steps[s]
-                x_waiting = transpose_x(c, t, h)
-                if c + 1 < n_chunks:
-                    m = t * STEPS_PER_UNIT + h
-                    if m == 0:
-                        new_w_tiles(c + 1)
-                    for n in range(m * W_BANKS, (m + 1) * W_BANKS):
-                        w_waiting.append((c + 1, n, transpose_w(c + 1, n)))
-                if t % 2 == 1 and h == STEPS_PER_UNIT - 1:
-                    n_free = min(len(stream), position[("x", c, t)] + 1 + RAW_BUFS)
-                    for n in range(n_loaded, n_free):
-                        raws[stream[n]] = load(stream[n])
-                    n_loaded = max(n_loaded, n_free)
+                slab, t = steps[s]
+                x_waiting = transpose_x(slab, t)
+                if s + LEAD < n_steps:
+                    w_slab, j, b = w_banks[s + LEAD]
+                    w_waiting.append((w_slab, j, b, transpose_w(w_slab, j, b)))
+                while n_loaded < len(stream) and last_use[stream[n_loaded - RAW_BUFS]] <= s:
+                    raws[stream[n_loaded]] = load(stream[n_loaded])
+                    n_loaded += 1
 
             if s >= LAG:
-                c_old, t_old, h_old = steps[s - LAG]
-                multiply(c_old, t_old, h_old, *x_ready[s - LAG])
+                old_slab, old_t = steps[s - LAG]
+                multiply(old_slab, old_t, *x_ready[s - LAG])
 
-            if s < n_steps and h == 0:
-                prepare_blend(c, t)
-            if s >= LAG and c_old == n_chunks - 1 and h_old == STEPS_PER_UNIT - 1:
-                blend_and_store(t_old)
+            if s < n_steps:
+                prepare_blend(slab, t)
+            if s >= LAG and old_slab == n_slabs - 1:
+                blend_and_store(old_t)

from contextlib import ExitStack

import concourse.mybir as mybir
from concourse.masks import make_identity

FLOPS = 2 * 512 * 256 * 16384

F32 = mybir.dt.float32
BF16 = mybir.dt.bfloat16
U32 = mybir.dt.uint32
U8 = mybir.dt.uint8
FP8X4 = mybir.dt.float8_e4m3fn_x4
ALU = mybir.AluOpType
ACT = mybir.ActivationFunctionType

P = 128
K_PASS = 512
K_BLOCK = 256
BANK = 512
K_BANK = 4 * K_BLOCK
SLAB = 2048
SLAB_PASSES = SLAB // K_PASS
UNIT_BANKS = SLAB // K_BANK
LAG = 2
LEAD = 2
RAW_BUFS = 24


def tile_persistentgrucell_pb_k_kernel(
    tc,
    x,
    rh,
    update,
    hidden,
    Wn,
    bn,
    connection_strength,
    connection_decay,
    connection_history,
    out,
):
    nc = tc.nc
    B, I = x.shape
    H = rh.shape[1]
    K = I + H
    ROW_TILES = B // P
    W_TILES = H // P
    n_slabs = K // SLAB
    assert n_slabs > 3

    x_rows = x.rearrange("(p t) k -> t p k", t=ROW_TILES)
    out_rows = out.rearrange("(p t) h -> t p h", t=ROW_TILES)

    steps = [(slab, t) for slab in range(n_slabs) for t in range(ROW_TILES)]
    w_banks = [
        (slab, j, b) for slab in range(n_slabs) for j in range(W_TILES) for b in range(UNIT_BANKS)
    ]
    n_steps = len(steps)
    assert len(w_banks) == n_steps
    assert W_TILES * UNIT_BANKS - 1 - LEAD + 1 <= LAG

    stream = []
    last_use = {}
    for i in range(LEAD):
        slab, j, b = w_banks[i]
        if b == 0:
            stream.append(("w", slab, j))
        last_use[("w", slab, j)] = -1
    for s in range(n_steps):
        if s + LEAD < n_steps:
            slab, j, b = w_banks[s + LEAD]
            if b == 0:
                stream.append(("w", slab, j))
            last_use[("w", slab, j)] = s
        slab, t = steps[s]
        stream.append(("x", slab, t))
        last_use[("x", slab, t)] = s

    with ExitStack() as ctx:
        ctx.enter_context(tc.manual_schedule())
        const = ctx.enter_context(tc.tile_pool(name="const", bufs=1))
        raw_pool = ctx.enter_context(tc.tile_pool(name="raw", bufs=RAW_BUFS))
        stage = ctx.enter_context(tc.tile_pool(name="stage", bufs=LAG + 2))
        w_pool = ctx.enter_context(tc.tile_pool(name="wq", bufs=3))
        out_pool = ctx.enter_context(tc.tile_pool(name="outs", bufs=2))
        acc_pool = ctx.enter_context(tc.psum_pool(name="acc", bufs=1))
        bank_pool = ctx.enter_context(tc.psum_pool(name="banks", bufs=4))

        def load(unit):
            kind, slab, r = unit
            raw = raw_pool.tile([P, SLAB], BF16, tag="raw")
            k0 = slab * SLAB
            if kind == "w":
                nc.sync.dma_start(out=raw[:], in_=Wn[r * P : (r + 1) * P, k0 : k0 + SLAB])
            else:
                width = min(SLAB, I - k0)
                nc.sync.dma_start(out=raw[:, 0:width], in_=x_rows[r][:, k0 : k0 + width])
            return raw

        ident = const.tile([P, P], F32)
        make_identity(nc, ident[:])
        ones = const.tile([P, P], BF16)
        nc.vector.memset(ones[:], 1.0)
        vectors = const.tile([P, 2 * BANK], BF16)
        nc.vector.memset(vectors[:], 0.0)
        zero = const.tile([P, 1], F32)
        nc.vector.memset(zero[:], 0.0)

        raws = {}
        raws[stream[0]] = load(stream[0])
        hid = const.tile([P, ROW_TILES * H], BF16)
        nc.scalar.dma_start(out=hid[:], in_=hidden.rearrange("(p t) h -> p (t h)", t=ROW_TILES))
        nc.scalar.dma_start(out=vectors[0:1, 0:H], in_=bn.unsqueeze(0))
        nc.scalar.dma_start(out=vectors[0:1, H : 2 * H], in_=connection_strength.unsqueeze(0))
        nc.scalar.dma_start(out=vectors[0:1, BANK : BANK + H], in_=connection_history.unsqueeze(0))
        nc.scalar.dma_start(
            out=vectors[0:1, BANK + H : BANK + H + 1], in_=connection_decay.unsqueeze(0)
        )
        for i in range(1, 4):
            raws[stream[i]] = load(stream[i])
        upd = const.tile([P, ROW_TILES * H], BF16)
        nc.scalar.dma_start(out=upd[:], in_=update.rearrange("(p t) h -> p (t h)", t=ROW_TILES))
        for i in range(4, RAW_BUFS):
            raws[stream[i]] = load(stream[i])
        rh_sb = const.tile([P, ROW_TILES * H], BF16)
        nc.sync.dma_start(out=rh_sb[:], in_=rh.rearrange("(p t) c -> p (t c)", t=ROW_TILES))

        warm = const.tile([P, 1], F32)
        nc.scalar.activation(out=warm[:], in_=zero[:], func=ACT.Sigmoid)

        habs = const.tile([P, ROW_TILES * H], BF16)
        nc.vector.scalar_tensor_tensor(
            out=habs[:], in0=hid[:], scalar=-1.0, in1=hid[:], op0=ALU.mult, op1=ALU.max
        )
        spread_a = acc_pool.tile([P, BANK], F32, tag="acc0")
        nc.tensor.matmul(spread_a[:], lhsT=ones[:], rhs=vectors[:, 0:BANK], start=True, stop=True)
        spread_b = acc_pool.tile([P, BANK], F32, tag="acc1")
        nc.tensor.matmul(
            spread_b[:], lhsT=ones[:], rhs=vectors[:, BANK : 2 * BANK], start=True, stop=True
        )
        abs_sum = acc_pool.tile([P, H], F32, tag="acc2")
        for t in range(ROW_TILES):
            nc.tensor.matmul(
                abs_sum[:],
                lhsT=ones[:],
                rhs=habs[:, t * H : (t + 1) * H],
                start=(t == 0),
                stop=(t == ROW_TILES - 1),
            )
        keep = const.tile([P, ROW_TILES * H], F32)
        nc.vector.tensor_tensor(out=keep[:], in0=upd[:], in1=hid[:], op=ALU.mult)
        nc.vector.tensor_tensor(out=keep[:], in0=hid[:], in1=keep[:], op=ALU.subtract)
        decay = const.tile([P, 1], F32)
        nc.vector.tensor_copy(out=decay[:], in_=spread_b[:, H : H + 1])
        ch = const.tile([P, H], F32)
        nc.vector.tensor_scalar(
            out=ch[:], in0=spread_b[:, 0:H], scalar1=decay[:, 0:1], scalar2=None, op0=ALU.mult
        )
        nc.vector.scalar_tensor_tensor(
            out=ch[:], in0=abs_sum[:], scalar=1.0 / B, in1=ch[:], op0=ALU.mult, op1=ALU.add
        )
        sig = const.tile([P, H], F32)
        nc.scalar.activation(out=sig[:], in_=ch[:], func=ACT.Sigmoid)
        cs = const.tile([P, H], F32)
        nc.vector.tensor_tensor(out=cs[:], in0=sig[:], in1=spread_a[:, H : 2 * H], op=ALU.mult)
        cs_bn = const.tile([P, H], F32)
        nc.vector.tensor_tensor(out=cs_bn[:], in0=cs[:], in1=spread_a[:, 0:H], op=ALU.mult)

        gain = const.tile([P, ROW_TILES * H], F32)
        bias = const.tile([P, ROW_TILES * H], F32)

        def prepare_blend(step, t):
            cols = slice(t * H, (t + 1) * H)
            if step == 0:
                nc.vector.tensor_tensor(out=gain[:, cols], in0=upd[:, cols], in1=cs[:], op=ALU.mult)
            elif step == 1:
                nc.vector.tensor_tensor(out=bias[:, cols], in0=upd[:, cols], in1=cs_bn[:], op=ALU.mult)
            elif step == 2:
                nc.vector.tensor_tensor(
                    out=keep[:, cols], in0=keep[:, cols], in1=bias[:, cols], op=ALU.add
                )

        acc = [
            acc_pool.tile([P, H], F32, name="acc%d" % t, tag="acc%d" % t) for t in range(ROW_TILES)
        ]

        def transpose_bank(blocks, grouped, on_vector):
            bank = bank_pool.tile([P, BANK], F32, tag="bank")
            for q in range(4):
                nc.tensor.transpose(bank[:, q * P : (q + 1) * P], blocks[q], ident[:])
            regrouped = bank[:].rearrange("p (g u r) -> p g r u", g=2, u=2)
            words = grouped.bitcast(F32).rearrange("p (g r u) -> p g r u", g=2, u=2)
            if on_vector:
                nc.vector.tensor_copy(out=words, in_=regrouped)
            else:
                nc.scalar.copy(out=words, in_=regrouped)

        def blocks_of(unit):
            kind, slab, r = unit
            words = raws[unit][:].bitcast(F32)
            blocks = [words[:, q * P : (q + 1) * P] for q in range(SLAB // K_BLOCK)]
            if kind == "x" and (slab + 1) * SLAB > I:
                blocks[-1] = rh_sb[:].bitcast(F32)[:, r * P : (r + 1) * P]
            return blocks

        def transpose_x(slab, t):
            blocks = blocks_of(("x", slab, t))
            x_grouped = stage.tile([P, SLAB], BF16, align_bytes=64)
            for b in range(UNIT_BANKS):
                transpose_bank(
                    blocks[4 * b : 4 * b + 4], x_grouped[:, b * K_BANK : (b + 1) * K_BANK], False
                )
            return x_grouped

        def transpose_w(slab, j, b):
            w_grouped = stage.tile([P, K_BANK], BF16, align_bytes=64)
            transpose_bank(blocks_of(("w", slab, j))[4 * b : 4 * b + 4], w_grouped[:], b % 2 == 1)
            return w_grouped

        w_codes = {}
        w_scales = {}

        def quantise_w(slab, j, b, w_grouped):
            if j == 0 and b == 0:
                codes = w_pool.tile([P, SLAB_PASSES * H], U32, align_bytes=64, tag="w_codes")
                scales = w_pool.tile([P, SLAB_PASSES * H], U8, align_bytes=64, tag="w_scales")
                w_codes[slab] = codes
                w_scales[slab] = scales
            for g in range(2):
                first = ((2 * b + g) * W_TILES + j) * P
                nc.vector.quantize_mx(
                    out=w_codes[slab][:, first : first + P].bitcast(FP8X4),
                    scales=w_scales[slab][:, first : first + P],
                    in_=w_grouped[:, g * 4 * P : (g + 1) * 4 * P],
                )

        def quantise_x(x_grouped):
            x_codes = stage.tile([P, SLAB // 4], U32, align_bytes=64)
            x_scales = stage.tile([P, SLAB // 4], U8, align_bytes=64)
            nc.vector.quantize_mx(out=x_codes[:].bitcast(FP8X4), scales=x_scales[:], in_=x_grouped[:])
            return x_codes, x_scales

        def multiply(slab, t, x_codes, x_scales):
            for g in range(SLAB_PASSES):
                nc.tensor.matmul_mx(
                    out=acc[t][:],
                    lhsT=x_codes[:, g * P : (g + 1) * P].bitcast(FP8X4),
                    lhsT_scale=x_scales[:, g * P : (g + 1) * P],
                    rhs=w_codes[slab][:, g * H : (g + 1) * H].bitcast(FP8X4),
                    rhs_scale=w_scales[slab][:, g * H : (g + 1) * H],
                    start=(slab == 0 and g == 0),
                    stop=(slab == n_slabs - 1 and g == SLAB_PASSES - 1),
                )

        def blend_and_store(t):
            cols = slice(t * H, (t + 1) * H)
            result = out_pool.tile([P, H], F32, tag="result")
            nc.vector.tensor_tensor(out=result[:], in0=acc[t][:], in1=gain[:, cols], op=ALU.mult)
            nc.vector.tensor_tensor(out=result[:], in0=result[:], in1=keep[:, cols], op=ALU.add)
            nc.sync.dma_start(out=out_rows[t], in_=result[:])

        w_waiting = [(slab, j, b, transpose_w(slab, j, b)) for slab, j, b in w_banks[0:LEAD]]
        x_waiting = None
        x_ready = {}
        n_loaded = RAW_BUFS
        for s in range(n_steps + LAG):
            if x_waiting is not None:
                x_ready[s - 1] = quantise_x(x_waiting)
                x_waiting = None
            for item in w_waiting:
                quantise_w(*item)
            w_waiting = []

            if s < n_steps:
                slab, t = steps[s]
                x_waiting = transpose_x(slab, t)
                if s + LEAD < n_steps:
                    w_slab, j, b = w_banks[s + LEAD]
                    w_waiting.append((w_slab, j, b, transpose_w(w_slab, j, b)))
                while n_loaded < len(stream) and last_use[stream[n_loaded - RAW_BUFS]] <= s:
                    raws[stream[n_loaded]] = load(stream[n_loaded])
                    n_loaded += 1

            if s >= LAG:
                old_slab, old_t = steps[s - LAG]
                multiply(old_slab, old_t, *x_ready[s - LAG])

            if s < n_steps:
                prepare_blend(slab, t)
            if s >= LAG and old_slab == n_slabs - 1:
                blend_and_store(old_t)
